import numpy as np
import ml_dtypes


def mxq(x, axis, fmt="e4m3"):
    dtype, down = {"e4m3": (ml_dtypes.float8_e4m3fn, 7), "e5m2": (ml_dtypes.float8_e5m2, 14)}[fmt]
    v = np.moveaxis(np.asarray(x, np.float32).astype(ml_dtypes.bfloat16).astype(np.float64), axis, -1)
    blocks = v.reshape(v.shape[:-1] + (-1, 32))
    amax = np.abs(blocks).max(-1, keepdims=True)
    byte = np.maximum(np.where(amax > 0, np.frexp(amax)[1] - 1 + 127, 0) - down, 1)
    scale = np.exp2(byte - 127.0)
    codes = (blocks / scale).astype(np.float32).astype(dtype).astype(np.float64)
    return np.moveaxis((codes * scale).reshape(v.shape), -1, axis)


WIDE = False


def mx_kscale(k):
    if not WIDE:
        return np.ones(k)
    levels = np.array([10, -10, 5, -5, 0])
    if k % 512:
        return np.exp2(np.random.permutation(np.resize(levels, k // 32))).repeat(32)
    a = np.empty((k // 512, 16))
    for p in range(k // 512):
        a[p, :8] = np.random.permutation(np.resize(levels, 8))
        for g in range(8):
            far = levels[np.abs(levels - a[p, g]) >= 10]
            a[p, g + 8] = far[np.random.randint(len(far))]
    return np.exp2(a.ravel()).repeat(32)


BF16 = ml_dtypes.bfloat16


def bf(x):
    return np.asarray(x, np.float32).astype(BF16)


def f64(x):
    return np.asarray(x).astype(np.float64)


B, HEADS, CH, H, W, HSP, WSP = 2, 6, 128, 32, 64, 16, 32
C = HEADS * CH
U, V = H // HSP, W // WSP
NW = U * V
N = HSP * WSP


def _vid2win(x):
    x = x.reshape(B, HEADS, CH, U, HSP, V, WSP)
    x = x.transpose(0, 3, 5, 1, 4, 6, 2)
    return x.reshape(B * NW, HEADS, N, CH)


def setup_inputs():
    s = mx_kscale(N)
    sp = np.tile(s.reshape(HSP, WSP), (U, V))
    kv = np.random.standard_normal((2, B, C, H, W))
    kv[1] = kv[1] / sp * s.max()
    q = np.random.standard_normal((B, C, H, W)) * 1.5
    mask = np.random.standard_normal((NW, N, N)) + np.log(s)[None, None, :]
    return {"kv": bf(kv), "q": bf(q), "mask": bf(mask)}


def reference(kv, q, mask):
    kv = f64(kv)
    k, v = kv[0], kv[1]
    qw = _vid2win(f64(q))
    kw = _vid2win(k)
    vw = _vid2win(v)
    attn = (qw @ kw.transpose(0, 1, 3, 2)) * CH ** (-0.5)
    attn = attn.reshape(B, NW, HEADS, N, N) + f64(mask)[None, :, None]
    attn = attn.reshape(B * NW, HEADS, N, N)
    e = np.exp(attn - attn.max(-1, keepdims=True))
    x = (mxq(e, 3, "e4m3") @ mxq(vw, 2, "e4m3")) / e.sum(-1, keepdims=True)
    x = x.reshape(B, U, V, HEADS, HSP, WSP, CH)
    x = x.transpose(0, 3, 6, 1, 4, 2, 5)
    return x.reshape(B, C, H, W)

@@ -1,0 +1,414 @@
+import math
+from contextlib import ExitStack
+
+import concourse.mybir as mybir
+from concourse.masks import make_identity
+
+F32 = mybir.dt.float32
+BF16 = mybir.dt.bfloat16
+U32 = mybir.dt.uint32
+U8 = mybir.dt.uint8
+FP8X4 = mybir.dt.float8_e4m3fn_x4
+AF = mybir.ActivationFunctionType
+ALU = mybir.AluOpType
+AX = mybir.AxisListType
+
+P = 128
+NB, HEADS, NWIN, N = 2, 6, 4, 512
+NBD = NB * HEADS
+NBLK = 2 * NBD
+NUNITS = 2 * NBLK
+HPIX = 1024
+SQRT_CH = math.sqrt(128.0)
+SCALE = 1.0 / SQRT_CH
+FLOPS = NUNITS * 2 * (2 * N * N * P)
+
+MANUAL = True
+ALL = (0, 1, 2, 3)
+S_SB_BUFS = 8
+FUSED_MAX = True
+DMA_WINDOWS = ('q', 'v')
+VE_ON_ACT = True
+DVE_MASK = ()
+OE_ON_ACT = ()
+
+
+def tile_window_attention_kernel(tc, kv, q, mask, out):
+    nc = tc.nc
+    q_v = q.rearrange("b (d c) (u h) w -> u (b d) c (h w)", c=P, u=2)
+    kv_v = kv.rearrange("s b (d c) (u h) w -> s u (b d) c (h w)", c=P, u=2)
+    out_v = out.rearrange("b (d c) (u h) w -> u (b d) c (h w)", c=P, u=2)
+    mask_v = mask.rearrange("w (j p) k -> w p j k", p=P)
+
+    with ExitStack() as ctx:
+        const = ctx.enter_context(tc.tile_pool(name="const", bufs=1))
+        raw = ctx.enter_context(tc.tile_pool(name="raw", bufs=4))
+        mraw = ctx.enter_context(tc.tile_pool(name="mraw", bufs=4))
+        win = ctx.enter_context(tc.tile_pool(name="win", bufs=4))
+        vq = ctx.enter_context(tc.tile_pool(name="vq", bufs=4))
+        small = ctx.enter_context(tc.tile_pool(name="small", bufs=16))
+        epool = ctx.enter_context(tc.tile_pool(name="epool", bufs=8))
+        spool = ctx.enter_context(tc.tile_pool(name="spool", bufs=S_SB_BUFS))
+        gpool = ctx.enter_context(tc.tile_pool(name="gpool", bufs=4))
+        opool = ctx.enter_context(tc.tile_pool(name="opool", bufs=3))
+        ps_s = ctx.enter_context(tc.psum_pool(name="ps_s", bufs=4))
+        ps_t = ctx.enter_context(tc.psum_pool(name="ps_t", bufs=2))
+        ps_o = ctx.enter_context(tc.psum_pool(name="ps_o", bufs=1))
+        if MANUAL:
+            ctx.enter_context(tc.manual_schedule())
+
+        ident_b = const.tile([P, P], BF16, name="ident_b")
+        ident_f = const.tile([P, P], F32, name="ident_f")
+        make_identity(nc, ident_b[:])
+        make_identity(nc, ident_f[:])
+        mask_t = const.tile([P, NWIN, 4, N], F32, name="mask_t")
+
+        blk_t = {}
+        unit = {}
+        chunk = {}
+
+        def load_mask(w):
+            m_sb = mraw.tile([P, 4, N], BF16, name="m_sb")
+            nc.sync.dma_start(out=m_sb[:], in_=mask_v[w])
+            blk_t[("m", w)] = m_sb
+
+        def mask_transposes(w, half):
+            m_sb = blk_t[("m", w)]
+            mt = ps_t.tile([P, 2, N], BF16, name="mt", tag="tr")
+            for ti in range(2):
+                for j in range(4):
+                    t = 2 * half + ti
+                    nc.tensor.transpose(mt[:, ti, j * P:(j + 1) * P], m_sb[:, j, t * P:(t + 1) * P], ident_b[:])
+            blk_t[("mt", w, half)] = mt
+
+        def mask_scale(w, half, on_scalar):
+            dst = mask_t[:, w, 2 * half:2 * half + 2, :]
+            src = blk_t[("mt", w, half)][:]
+            if on_scalar:
+                nc.scalar.mul(out=dst, in_=src, mul=SQRT_CH)
+            else:
+                nc.vector.tensor_scalar_mul(out=dst, in0=src, scalar1=SQRT_CH)
+
+        def load_one(what, blk, vws=(0, 1)):
+            uw, bd = blk // NBD, blk % NBD
+            src = {"q": q_v[uw, bd], "k": kv_v[0, uw, bd], "v": kv_v[1, uw, bd]}[what]
+            if what in DMA_WINDOWS:
+                if 0 in vws:
+                    blk_t[(what + "_win", blk)] = win.tile([P, 2, N], BF16, name=what + "_win")
+                for vw in vws:
+                    nc.sync.dma_start(
+                        out=blk_t[(what + "_win", blk)][:, vw, :].rearrange("c (h w) -> c h w", h=16),
+                        in_=src.rearrange("c (h v w) -> c h v w", h=16, v=2)[:, :, vw, :],
+                    )
+            else:
+                t = raw.tile([P, HPIX], BF16, name=what + "_raw")
+                nc.sync.dma_start(out=t[:], in_=src)
+                blk_t[(what + "_raw", blk)] = t
+
+        def load_blk(blk):
+            for what in ("q", "k", "v"):
+                load_one(what, blk)
+
+        def to_windows(what, blk):
+            if what in DMA_WINDOWS:
+                return
+            dst = win.tile([P, 2, N], BF16, name=what + "_win")
+            nc.vector.tensor_copy(
+                out=dst[:].rearrange("c v (h w) -> c v h w", h=16),
+                in_=blk_t[(what + "_raw", blk)][:].rearrange("c (h v w) -> c v h w", h=16, v=2),
+            )
+            blk_t[(what + "_win", blk)] = dst
+
+        def v_transposes(blk):
+            v_win = blk_t[("v_win", blk)]
+            vt = ps_t.tile([P, 2, 2, P], F32, name="vt", tag="tr")
+            for vw in range(2):
+                for u in range(2):
+                    nc.tensor.transpose(vt[:, vw, u, :], v_win[:, vw, :].bitcast(F32)[:, u::2], ident_f[:])
+            blk_t[("vt", blk)] = vt
+
+        def v_regroup(blk, on_scalar):
+            vg = vq.tile([P, 2, P, 4], BF16, name="vg", align_bytes=64)
+            src = blk_t[("vt", blk)][:].rearrange("p w u c -> p w c u")
+            if on_scalar:
+                nc.scalar.copy(out=vg[:].bitcast(F32), in_=src)
+            else:
+                nc.vector.tensor_copy(out=vg[:].bitcast(F32), in_=src)
+            blk_t[("vg", blk)] = vg
+
+        def quantise_v(blk):
+            v_codes = vq.tile([P, 2 * P], U32, name="v_codes", align_bytes=64)
+            v_scl = vq.tile([P, 2 * P], U8, name="v_scl", align_bytes=64)
+            nc.vector.quantize_mx(
+                out=v_codes[:].bitcast(FP8X4),
+                scales=v_scl[:],
+                in_=blk_t[("vg", blk)][:].rearrange("p w c t -> p (w c t)"),
+            )
+            blk_t[("v_codes", blk)] = v_codes
+            blk_t[("v_scl", blk)] = v_scl
+
+        def add_mask(n, j):
+            w = 2 * (n // 2 // NBD) + n % 2
+            s_ps = ps_s.tile([P, N], F32, name="s_ps")
+            chunk[("s", n, j)] = s_ps
+            for t in range(4):
+                nc.tensor.matmul(
+                    out=s_ps[:, t * P:(t + 1) * P],
+                    lhsT=mask_t[:, w, t, j * P:(j + 1) * P],
+                    rhs=ident_f[:],
+                    is_transpose=True,
+                    start=(t == 0),
+                    stop=False,
+                )
+
+        def add_qk(n, j):
+            blk, vw = n // 2, n % 2
+            nc.tensor.matmul(
+                out=chunk[("s", n, j)][:],
+                lhsT=blk_t[("q_win", blk)][:, vw, j * P:(j + 1) * P],
+                rhs=blk_t[("k_raw", blk)][:].rearrange("c (h v x) -> c h v x", h=16, v=2)[:, :, vw, :],
+                start=False,
+                stop=True,
+            )
+
+        def row_max(n, j):
+            w = 2 * (n // 2 // NBD) + n % 2
+            src = chunk[("s", n, j)]
+            nb = small.tile([P, 1], F32, name="nb")
+            if j in DVE_MASK:
+                s_sb = spool.tile([P, N], F32, name="s_sb")
+                nc.vector.scalar_tensor_tensor(out=s_sb[:], in0=src[:], scalar=SCALE, in1=blk_t[("m", w)][:, j, :],
+                                               op0=ALU.mult, op1=ALU.add)
+                chunk[("s", n, j)] = s_sb
+                nc.vector.tensor_reduce(out=nb[:], in_=s_sb[:], axis=AX.X, op=ALU.max, negate=True)
+            elif FUSED_MAX:
+                s_neg = spool.tile([P, N], F32, name="s_neg")
+                nc.vector.tensor_scalar(out=s_neg[:], in0=src[:], scalar1=-SCALE, scalar2=None, op0=ALU.mult,
+                                        op1=ALU.min, accum_out=nb[:])
+                chunk[("s", n, j)] = s_neg
+            else:
+                nm = small.tile([P, 1], F32, name="nm")
+                nc.vector.tensor_reduce(out=nm[:], in_=src[:], axis=AX.X, op=ALU.max, negate=True)
+                nc.vector.tensor_scalar_mul(out=nb[:], in0=nm[:], scalar1=SCALE)
+            chunk[("nb", n, j)] = nb[:]
+
+        def exps(n, half):
+            if half == 0 and n % 2 == 0:
+                blk_t[("rs", n // 2)] = small.tile([P, 8], F32, name="rs")
+            for i in range(2):
+                j = 2 * half + i
+                e_sb = epool.tile([P, N], BF16, name="e_sb")
+                nc.scalar.activation(
+                    out=e_sb[:].rearrange("p (u m r) -> p u m r", u=2, r=2),
+                    in_=chunk[("s", n, j)][:].rearrange("p (m u r) -> p u m r", u=2, r=2),
+                    func=AF.Exp,
+                    bias=chunk[("nb", n, j)],
+                    scale=(1.0 if j in DVE_MASK else -1.0),
+                    accum_out=blk_t[("rs", n // 2)][:, 4 * (n % 2) + j:4 * (n % 2) + j + 1],
+                )
+                chunk[("e", n, j)] = e_sb
+
+        def e_transposes(n, half):
+            et = ps_t.tile([P, 2, 256], F32, name="et", tag="tr")
+            for i in range(2):
+                e_sb = chunk[("e", n, 2 * half + i)]
+                for u in range(2):
+                    nc.tensor.transpose(et[:, u, i * P:(i + 1) * P], e_sb[:].bitcast(F32)[:, u * P:(u + 1) * P],
+                                        ident_f[:])
+            unit[("et", n, half)] = et
+
+        def regroup(n, half):
+            if half == 0:
+                unit[("g", n)] = gpool.tile([P, N, 4], BF16, name="grp", align_bytes=64)
+            nc.scalar.copy(
+                out=unit[("g", n)][:, 256 * half:256 * half + 256, :].bitcast(F32),
+                in_=unit[("et", n, half)][:].rearrange("p u q -> p q u"),
+            )
+
+        def quantise_e(n, js):
+            if js[0] == 0:
+                unit[("codes", n)] = gpool.tile([P, N], U32, name="codes", align_bytes=64)
+                unit[("scl", n)] = gpool.tile([P, N], U8, name="scl", align_bytes=64)
+            lo, hi = js[0] * P, (js[-1] + 1) * P
+            nc.vector.quantize_mx(
+                out=unit[("codes", n)][:, lo:hi].bitcast(FP8X4),
+                scales=unit[("scl", n)][:, lo:hi],
+                in_=unit[("g", n)][:, lo:hi, :].rearrange("p q t -> p (q t)"),
+            )
+
+        def mx_passes(n, js, spare=False):
+            blk, vw = n // 2, n % 2
+            if spare:
+                o_ps = ps_s.tile([P, 4, P], F32, name="o_ps", tag="s_ps")
+            else:
+                o_ps = ps_o.tile([P, 4, P], F32, name="o_ps")
+            for j in js:
+                nc.tensor.matmul_mx(
+                    out=o_ps[:, j, :],
+                    lhsT=unit[("codes", n)][:, j * P:(j + 1) * P].bitcast(FP8X4),
+                    lhsT_scale=unit[("scl", n)][:, j * P:(j + 1) * P],
+                    rhs=blk_t[("v_codes", blk)][:, vw * P:(vw + 1) * P].bitcast(FP8X4),
+                    rhs_scale=blk_t[("v_scl", blk)][:, vw * P:(vw + 1) * P],
+                    start=True,
+                    stop=True,
+                )
+            unit[("o_ps", n, js[0])] = o_ps
+
+        def normalise(n, js):
+            blk, vw = n // 2, n % 2
+            if vw == 0:
+                rinv = small.tile([P, 8], F32, name="rinv")
+                nc.vector.reciprocal(out=rinv[:], in_=blk_t[("rs", blk)][:])
+                blk_t[("rinv", blk)] = rinv
+            lo, hi = js[0], js[-1] + 1
+            o_sb = opool.tile([P, 4, P], F32, name="o_sb")
+            nc.vector.tensor_tensor(
+                out=o_sb[:, lo:hi, :],
+                in0=unit[("o_ps", n, lo)][:, lo:hi, :],
+                in1=blk_t[("rinv", blk)][:, 4 * vw + lo:4 * vw + hi].unsqueeze(2).to_broadcast([P, hi - lo, P]),
+                op=ALU.mult,
+            )
+            unit[("o_sb", n, lo)] = o_sb
+
+        def o_transposes(n, js, spare=False):
+            if spare:
+                ot = ps_s.tile([P, N], F32, name="ot", tag="s_ps")
+            else:
+                ot = ps_o.tile([P, N], F32, name="ot")
+            for j in js:
+                nc.tensor.transpose(ot[:, j * P:(j + 1) * P], unit[("o_sb", n, js[0])][:, j, :], ident_f[:])
+            unit[("ot", n, js[0])] = ot
+
+        def o_out(n, js, on_scalar):
+            blk, vw = n // 2, n % 2
+            if vw == 0:
+                blk_t[("out", blk)] = opool.tile([P, HPIX], F32, name="out_sb")
+            out_sb = blk_t[("out", blk)]
+            h0, h1 = 4 * js[0], 4 * (js[-1] + 1)
+            dst = out_sb[:].rearrange("c (h v x) -> c h v x", h=16, v=2)[:, h0:h1, vw, :]
+            src = unit[("ot", n, js[0])][:, js[0] * P:(js[-1] + 1) * P].rearrange("c (h x) -> c h x", x=32)
+            if on_scalar:
+                nc.scalar.copy(out=dst, in_=src)
+            else:
+                nc.vector.tensor_copy(out=dst, in_=src)
+            if vw == 1 and js[-1] == 3:
+                nc.sync.dma_start(out=out_v[blk // NBD, blk % NBD], in_=out_sb[:])
+
+        def ok(n):
+            return 0 <= n < NUNITS
+
+        warm = const.tile([P, 1], F32, name="warm")
+        nc.vector.memset(warm[:], 0.0)
+        nc.scalar.activation(out=warm[:], in_=warm[:], func=AF.Exp)
+
+        load_mask(0)
+        load_one("q", 0, (0,))
+        load_one("k", 0)
+        load_one("q", 0, (1,))
+        load_mask(1)
+        load_one("v", 0)
+        load_blk(1)
+        load_blk(2)
+        load_mask(2)
+        load_mask(3)
+        for half in range(2):
+            mask_transposes(0, half)
+            mask_scale(0, half, half == 0)
+        to_windows("q", 0)
+
+        for m in range(NUNITS):
+            blk, vw = m // 2, m % 2
+            nxt = blk + 1
+            late_mask = {4: 2, 6: 3}.get(m)
+            if vw == 0 and 1 <= blk and blk + 2 < NBLK:
+                load_blk(blk + 2)
+            if ok(m):
+                add_mask(m, 0)
+                add_qk(m, 0)
+            if ok(m - 1):
+                e_transposes(m - 1, 0)
+                regroup(m - 1, 0)
+            if vw == 0 and 1 <= blk < NBLK:
+                v_regroup(blk, VE_ON_ACT)
+            if ok(m):
+                add_mask(m, 1)
+                add_qk(m, 1)
+                add_mask(m, 2)
+                add_mask(m, 3)
+                add_qk(m, 2)
+            if ok(m - 3):
+                mx_passes(m - 3, ALL)
+            if ok(m):
+                add_qk(m, 3)
+            if ok(m - 1):
+                e_transposes(m - 1, 1)
+            if ok(m - 4):
+                o_transposes(m - 4, ALL)
+            if m == 0:
+                mask_transposes(1, 0)
+            if vw == 1 and nxt < NBLK:
+                v_transposes(nxt)
+            if ok(m):
+                row_max(m, 0)
+                row_max(m, 1)
+            if ok(m - 2):
+                quantise_e(m - 2, ALL)
+            if ok(m):
+                row_max(m, 2)
+            if ok(m - 3):
+                normalise(m - 3, ALL)
+            if ok(m):
+                row_max(m, 3)
+            if m == 0:
+                to_windows("v", 0)
+            if vw == 0 and nxt < NBLK:
+                to_windows("v", nxt)
+                to_windows("q", nxt)
+            if vw == 0 and 1 <= blk < NBLK:
+                quantise_v(blk)
+            if late_mask is not None:
+                mask_transposes(late_mask, 0)
+                mask_scale(late_mask, 0, False)
+            if ok(m):
+                exps(m, 0)
+            if m == 0:
+                mask_scale(1, 0, True)
+                mask_transposes(1, 1)
+            if ok(m - 1):
+                regroup(m - 1, 1)
+            if late_mask is not None:
+                mask_transposes(late_mask, 1)
+                mask_scale(late_mask, 1, True)
+            if ok(m - 4):
+                o_out(m - 4, ALL, (m - 4) % 4 in OE_ON_ACT)
+            if ok(m):
+                exps(m, 1)
+            if m == 0:
+                mask_scale(1, 1, False)
+                v_transposes(0)
+                v_regroup(0, False)
+                quantise_v(0)
+
+        z = NUNITS - 1
+        first, second = (0, 1), (2, 3)
+        e_transposes(z, 0)
+        regroup(z, 0)
+        mx_passes(z - 2, ALL)
+        e_transposes(z, 1)
+        o_transposes(z - 3, ALL)
+        quantise_e(z - 1, ALL)
+        normalise(z - 2, ALL)
+        quantise_e(z, first)
+        regroup(z, 1)
+        quantise_e(z, second)
+        o_out(z - 3, ALL, True)
+        mx_passes(z - 1, ALL, True)
+        mx_passes(z, first, True)
+        o_transposes(z - 2, ALL)
+        o_out(z - 2, ALL, True)
+        mx_passes(z, second, True)
+        for n, js in ((z - 1, ALL), (z, first), (z, second)):
+            normalise(n, js)
+        for n, js in ((z - 1, ALL), (z, first), (z, second)):
+            o_transposes(n, js, True)
+            o_out(n, js, True)

@@ -27,10 +27,8 @@ MANUAL = True
 ALL = (0, 1, 2, 3)
 S_SB_BUFS = 8
 FUSED_MAX = True
-DMA_WINDOWS = ('q', 'v')
 VE_ON_ACT = True
 DVE_MASK = ()
-OE_ON_ACT = ()
 
 
 def tile_window_attention_kernel(tc, kv, q, mask, out):
@@ -38,22 +36,23 @@ def tile_window_attention_kernel(tc, kv, q, mask, out):
     q_v = q.rearrange("b (d c) (u h) w -> u (b d) c (h w)", c=P, u=2)
     kv_v = kv.rearrange("s b (d c) (u h) w -> s u (b d) c (h w)", c=P, u=2)
     out_v = out.rearrange("b (d c) (u h) w -> u (b d) c (h w)", c=P, u=2)
-    mask_v = mask.rearrange("w (j p) k -> w p j k", p=P)
+    mask_v = mask.rearrange("w (p j) k -> w p j k", j=4)
 
     with ExitStack() as ctx:
         const = ctx.enter_context(tc.tile_pool(name="const", bufs=1))
         raw = ctx.enter_context(tc.tile_pool(name="raw", bufs=4))
         mraw = ctx.enter_context(tc.tile_pool(name="mraw", bufs=4))
         win = ctx.enter_context(tc.tile_pool(name="win", bufs=4))
-        vq = ctx.enter_context(tc.tile_pool(name="vq", bufs=4))
+        vq = ctx.enter_context(tc.tile_pool(name="vq", bufs=5))
         small = ctx.enter_context(tc.tile_pool(name="small", bufs=16))
         epool = ctx.enter_context(tc.tile_pool(name="epool", bufs=8))
         spool = ctx.enter_context(tc.tile_pool(name="spool", bufs=S_SB_BUFS))
-        gpool = ctx.enter_context(tc.tile_pool(name="gpool", bufs=4))
+        gpool = ctx.enter_context(tc.tile_pool(name="gpool", bufs=5))
         opool = ctx.enter_context(tc.tile_pool(name="opool", bufs=3))
         ps_s = ctx.enter_context(tc.psum_pool(name="ps_s", bufs=4))
         ps_t = ctx.enter_context(tc.psum_pool(name="ps_t", bufs=2))
-        ps_o = ctx.enter_context(tc.psum_pool(name="ps_o", bufs=1))
+        rpool = ctx.enter_context(tc.tile_pool(name="rpool", bufs=4))
+        ps_o = ctx.enter_context(tc.psum_pool(name="ps_o", bufs=2))
         if MANUAL:
             ctx.enter_context(tc.manual_schedule())
 
@@ -89,42 +88,39 @@ def tile_window_attention_kernel(tc, kv, q, mask, out):
             else:
                 nc.vector.tensor_scalar_mul(out=dst, in0=src, scalar1=SQRT_CH)
 
-        def load_one(what, blk, vws=(0, 1)):
+        def load_one(what, blk):
             uw, bd = blk // NBD, blk % NBD
             src = {"q": q_v[uw, bd], "k": kv_v[0, uw, bd], "v": kv_v[1, uw, bd]}[what]
-            if what in DMA_WINDOWS:
-                if 0 in vws:
-                    blk_t[(what + "_win", blk)] = win.tile([P, 2, N], BF16, name=what + "_win")
-                for vw in vws:
-                    nc.sync.dma_start(
-                        out=blk_t[(what + "_win", blk)][:, vw, :].rearrange("c (h w) -> c h w", h=16),
-                        in_=src.rearrange("c (h v w) -> c h v w", h=16, v=2)[:, :, vw, :],
-                    )
-            else:
-                t = raw.tile([P, HPIX], BF16, name=what + "_raw")
-                nc.sync.dma_start(out=t[:], in_=src)
-                blk_t[(what + "_raw", blk)] = t
+            t = raw.tile([P, HPIX], BF16, name=what + "_raw")
+            nc.sync.dma_start(out=t[:], in_=src)
+            blk_t[(what + "_raw", blk)] = t
 
         def load_blk(blk):
             for what in ("q", "k", "v"):
                 load_one(what, blk)
 
-        def to_windows(what, blk):
-            if what in DMA_WINDOWS:
-                return
-            dst = win.tile([P, 2, N], BF16, name=what + "_win")
-            nc.vector.tensor_copy(
-                out=dst[:].rearrange("c v (h w) -> c v h w", h=16),
-                in_=blk_t[(what + "_raw", blk)][:].rearrange("c (h v w) -> c v h w", h=16, v=2),
-            )
-            blk_t[(what + "_win", blk)] = dst
+        def sort_q(blk, eng):
+            dst = win.tile([P, 2, 256], F32, name="q_words")
+            src = blk_t[("q_raw", blk)][:].bitcast(F32).rearrange("c (h v x) -> c v h x", h=16, v=2)
+            for vw in range(2):
+                for h in (slice(0, 8), slice(8, 16)):
+                    eng.tensor_copy(out=dst[:, vw, :].rearrange("c (h x) -> c h x", h=16)[:, h, :], in_=src[:, vw, h, :])
+            blk_t[("q_win", blk)] = dst[:].rearrange("c v n -> c (v n)").bitcast(BF16)
+
+        def sort_v(blk, eng):
+            dst = win.tile([P, 2, 2, P], F32, name="v_words")
+            src = blk_t[("v_raw", blk)][:].bitcast(F32).rearrange("c (h v x u) -> c v u h x", h=16, v=2, u=2)
+            for vw in range(2):
+                for u in range(2):
+                    eng.tensor_copy(out=dst[:, vw, u, :].rearrange("c (h x) -> c h x", h=16), in_=src[:, vw, u])
+            blk_t[("v_words", blk)] = dst
 
         def v_transposes(blk):
-            v_win = blk_t[("v_win", blk)]
+            v_words = blk_t[("v_words", blk)]
             vt = ps_t.tile([P, 2, 2, P], F32, name="vt", tag="tr")
             for vw in range(2):
                 for u in range(2):
-                    nc.tensor.transpose(vt[:, vw, u, :], v_win[:, vw, :].bitcast(F32)[:, u::2], ident_f[:])
+                    nc.tensor.transpose(vt[:, vw, u, :], v_words[:, vw, u, :], ident_f[:])
             blk_t[("vt", blk)] = vt
 
         def v_regroup(blk, on_scalar):
@@ -165,7 +161,7 @@ def tile_window_attention_kernel(tc, kv, q, mask, out):
             blk, vw = n // 2, n % 2
             nc.tensor.matmul(
                 out=chunk[("s", n, j)][:],
-                lhsT=blk_t[("q_win", blk)][:, vw, j * P:(j + 1) * P],
+                lhsT=blk_t[("q_win", blk)][:, vw * N + j:(vw + 1) * N:4],
                 rhs=blk_t[("k_raw", blk)][:].rearrange("c (h v x) -> c h v x", h=16, v=2)[:, :, vw, :],
                 start=False,
                 stop=True,
@@ -236,63 +232,57 @@ def tile_window_attention_kernel(tc, kv, q, mask, out):
                 in_=unit[("g", n)][:, lo:hi, :].rearrange("p q t -> p (q t)"),
             )
 
-        def mx_passes(n, js, spare=False):
+        def mx_pass(n):
             blk, vw = n // 2, n % 2
-            if spare:
-                o_ps = ps_s.tile([P, 4, P], F32, name="o_ps", tag="s_ps")
-            else:
-                o_ps = ps_o.tile([P, 4, P], F32, name="o_ps")
-            for j in js:
-                nc.tensor.matmul_mx(
-                    out=o_ps[:, j, :],
-                    lhsT=unit[("codes", n)][:, j * P:(j + 1) * P].bitcast(FP8X4),
-                    lhsT_scale=unit[("scl", n)][:, j * P:(j + 1) * P],
-                    rhs=blk_t[("v_codes", blk)][:, vw * P:(vw + 1) * P].bitcast(FP8X4),
-                    rhs_scale=blk_t[("v_scl", blk)][:, vw * P:(vw + 1) * P],
-                    start=True,
-                    stop=True,
-                )
-            unit[("o_ps", n, js[0])] = o_ps
-
-        def normalise(n, js):
-            blk, vw = n // 2, n % 2
-            if vw == 0:
-                rinv = small.tile([P, 8], F32, name="rinv")
-                nc.vector.reciprocal(out=rinv[:], in_=blk_t[("rs", blk)][:])
-                blk_t[("rinv", blk)] = rinv
-            lo, hi = js[0], js[-1] + 1
-            o_sb = opool.tile([P, 4, P], F32, name="o_sb")
-            nc.vector.tensor_tensor(
-                out=o_sb[:, lo:hi, :],
-                in0=unit[("o_ps", n, lo)][:, lo:hi, :],
-                in1=blk_t[("rinv", blk)][:, 4 * vw + lo:4 * vw + hi].unsqueeze(2).to_broadcast([P, hi - lo, P]),
-                op=ALU.mult,
+            o_ps = ps_o.tile([P, N], F32, name="o_ps")
+            nc.tensor.matmul_mx(
+                out=o_ps[:],
+                lhsT=blk_t[("v_codes", blk)][:, vw * P:(vw + 1) * P].bitcast(FP8X4),
+                lhsT_scale=blk_t[("v_scl", blk)][:, vw * P:(vw + 1) * P],
+                rhs=unit[("codes", n)][:].bitcast(FP8X4),
+                rhs_scale=unit[("scl", n)][:],
+                start=True,
+                stop=True,
             )
-            unit[("o_sb", n, lo)] = o_sb
+            unit[("o_ps", n)] = o_ps
 
-        def o_transposes(n, js, spare=False):
-            if spare:
-                ot = ps_s.tile([P, N], F32, name="ot", tag="s_ps")
-            else:
-                ot = ps_o.tile([P, N], F32, name="ot")
-            for j in js:
-                nc.tensor.transpose(ot[:, j * P:(j + 1) * P], unit[("o_sb", n, js[0])][:, j, :], ident_f[:])
-            unit[("ot", n, js[0])] = ot
+        def invert_sums(blk):
+            rinv = small.tile([P, 8], F32, name="rinv")
+            nc.vector.reciprocal(out=rinv[:], in_=blk_t[("rs", blk)][:])
+            blk_t[("rinv", blk)] = rinv
 
-        def o_out(n, js, on_scalar):
+        def spread_through_out(blk):
+            row = out_v[blk // NBD, blk % NBD, 0]
+            nc.sync.dma_start(out=row.rearrange("(p k) -> p k", k=8), in_=blk_t[("rinv", blk)][:])
+            r_sb = rpool.tile([P, HPIX], F32, name="r_sb")
+            nc.sync.dma_start(out=r_sb[:], in_=row.partition_broadcast(P))
+            blk_t[("r", blk)] = r_sb[:].rearrange("c (h y v j) -> c v h y j", h=16, y=8, v=2)
+
+        def spread_on_tensor(n):
+            blk, vw = n // 2, n % 2
+            r_ps = ps_s.tile([P, N], F32, name="r_ps", tag="s_ps")
+            for j in range(4):
+                k = 4 * vw + j
+                nc.tensor.transpose(r_ps[:, j * P:(j + 1) * P], blk_t[("rinv", blk)][:, k:k + 1].to_broadcast([P, P]), ident_f[:])
+            r_sb = rpool.tile([P, N], F32, name="r_one")
+            nc.scalar.copy(out=r_sb[:], in_=r_ps[:])
+            unit[("r", n)] = r_sb[:].rearrange("c (j h y) -> c h y j", j=4, h=16)
+
+        def normalise(n):
             blk, vw = n // 2, n % 2
             if vw == 0:
                 blk_t[("out", blk)] = opool.tile([P, HPIX], F32, name="out_sb")
             out_sb = blk_t[("out", blk)]
-            h0, h1 = 4 * js[0], 4 * (js[-1] + 1)
-            dst = out_sb[:].rearrange("c (h v x) -> c h v x", h=16, v=2)[:, h0:h1, vw, :]
-            src = unit[("ot", n, js[0])][:, js[0] * P:(js[-1] + 1) * P].rearrange("c (h x) -> c h x", x=32)
-            if on_scalar:
-                nc.scalar.copy(out=dst, in_=src)
-            else:
-                nc.vector.tensor_copy(out=dst, in_=src)
-            if vw == 1 and js[-1] == 3:
-                nc.sync.dma_start(out=out_v[blk // NBD, blk % NBD], in_=out_sb[:])
+            r = unit[("r", n)] if ("r", n) in unit else blk_t[("r", blk)][:, vw]
+            nc.vector.tensor_tensor(
+                out=out_sb[:].rearrange("c (h v y j) -> c v h y j", h=16, v=2, y=8)[:, vw],
+                in0=unit[("o_ps", n)][:].rearrange("c (j h y) -> c h y j", j=4, h=16),
+                in1=r,
+                op=ALU.mult,
+            )
+
+        def store(blk):
+            nc.sync.dma_start(out=out_v[blk // NBD, blk % NBD], in_=blk_t[("out", blk)][:])
 
         def ok(n):
             return 0 <= n < NUNITS
@@ -302,9 +292,8 @@ def tile_window_attention_kernel(tc, kv, q, mask, out):
         nc.scalar.activation(out=warm[:], in_=warm[:], func=AF.Exp)
 
         load_mask(0)
-        load_one("q", 0, (0,))
+        load_one("q", 0)
         load_one("k", 0)
-        load_one("q", 0, (1,))
         load_mask(1)
         load_one("v", 0)
         load_blk(1)
@@ -314,7 +303,7 @@ def tile_window_attention_kernel(tc, kv, q, mask, out):
         for half in range(2):
             mask_transposes(0, half)
             mask_scale(0, half, half == 0)
-        to_windows("q", 0)
+        sort_q(0, nc.vector)
 
         for m in range(NUNITS):
             blk, vw = m // 2, m % 2
@@ -322,6 +311,9 @@ def tile_window_attention_kernel(tc, kv, q, mask, out):
             late_mask = {4: 2, 6: 3}.get(m)
             if vw == 0 and 1 <= blk and blk + 2 < NBLK:
                 load_blk(blk + 2)
+            if vw == 0 and nxt < NBLK:
+                sort_v(nxt, nc.gpsimd)
+                sort_q(nxt, nc.gpsimd)
             if ok(m):
                 add_mask(m, 0)
                 add_qk(m, 0)
@@ -336,14 +328,12 @@ def tile_window_attention_kernel(tc, kv, q, mask, out):
                 add_mask(m, 2)
                 add_mask(m, 3)
                 add_qk(m, 2)
-            if ok(m - 3):
-                mx_passes(m - 3, ALL)
+            if ok(m - 4):
+                mx_pass(m - 4)
             if ok(m):
                 add_qk(m, 3)
             if ok(m - 1):
                 e_transposes(m - 1, 1)
-            if ok(m - 4):
-                o_transposes(m - 4, ALL)
             if m == 0:
                 mask_transposes(1, 0)
             if vw == 1 and nxt < NBLK:
@@ -355,15 +345,17 @@ def tile_window_attention_kernel(tc, kv, q, mask, out):
                 quantise_e(m - 2, ALL)
             if ok(m):
                 row_max(m, 2)
-            if ok(m - 3):
-                normalise(m - 3, ALL)
+            if vw == 0 and blk >= 1:
+                invert_sums(blk - 1)
+                spread_through_out(blk - 1)
+            if ok(m - 5):
+                normalise(m - 5)
+                if vw == 0:
+                    store((m - 5) // 2)
             if ok(m):
                 row_max(m, 3)
             if m == 0:
-                to_windows("v", 0)
-            if vw == 0 and nxt < NBLK:
-                to_windows("v", nxt)
-                to_windows("q", nxt)
+                sort_v(0, nc.vector)
             if vw == 0 and 1 <= blk < NBLK:
                 quantise_v(blk)
             if late_mask is not None:
@@ -379,8 +371,6 @@ def tile_window_attention_kernel(tc, kv, q, mask, out):
             if late_mask is not None:
                 mask_transposes(late_mask, 1)
                 mask_scale(late_mask, 1, True)
-            if ok(m - 4):
-                o_out(m - 4, ALL, (m - 4) % 4 in OE_ON_ACT)
             if ok(m):
                 exps(m, 1)
             if m == 0:
@@ -390,25 +380,26 @@ def tile_window_attention_kernel(tc, kv, q, mask, out):
                 quantise_v(0)
 
         z = NUNITS - 1
-        first, second = (0, 1), (2, 3)
+        last = NBLK - 1
         e_transposes(z, 0)
         regroup(z, 0)
-        mx_passes(z - 2, ALL)
+        mx_pass(z - 3)
         e_transposes(z, 1)
-        o_transposes(z - 3, ALL)
         quantise_e(z - 1, ALL)
-        normalise(z - 2, ALL)
-        quantise_e(z, first)
+        invert_sums(last)
+        normalise(z - 4)
+        store(last - 2)
+        mx_pass(z - 2)
+        quantise_e(z, (0, 1))
         regroup(z, 1)
-        quantise_e(z, second)
-        o_out(z - 3, ALL, True)
-        mx_passes(z - 1, ALL, True)
-        mx_passes(z, first, True)
-        o_transposes(z - 2, ALL)
-        o_out(z - 2, ALL, True)
-        mx_passes(z, second, True)
-        for n, js in ((z - 1, ALL), (z, first), (z, second)):
-            normalise(n, js)
-        for n, js in ((z - 1, ALL), (z, first), (z, second)):
-            o_transposes(n, js, True)
-            o_out(n, js, True)
+        normalise(z - 3)
+        quantise_e(z, (2, 3))
+        mx_pass(z - 1)
+        spread_on_tensor(z - 1)
+        spread_on_tensor(z)
+        normalise(z - 2)
+        store(last - 1)
+        mx_pass(z)
+        normalise(z - 1)
+        normalise(z)
+        store(last)

@@ -23,12 +23,8 @@ SQRT_CH = math.sqrt(128.0)
 SCALE = 1.0 / SQRT_CH
 FLOPS = NUNITS * 2 * (2 * N * N * P)
 
-MANUAL = True
 ALL = (0, 1, 2, 3)
-S_SB_BUFS = 8
-FUSED_MAX = True
-VE_ON_ACT = True
-DVE_MASK = ()
+VECTOR_MASK = (0,)
 
 
 def tile_window_attention_kernel(tc, kv, q, mask, out):
@@ -43,18 +39,17 @@ def tile_window_attention_kernel(tc, kv, q, mask, out):
         raw = ctx.enter_context(tc.tile_pool(name="raw", bufs=4))
         mraw = ctx.enter_context(tc.tile_pool(name="mraw", bufs=4))
         win = ctx.enter_context(tc.tile_pool(name="win", bufs=4))
-        vq = ctx.enter_context(tc.tile_pool(name="vq", bufs=5))
+        vq = ctx.enter_context(tc.tile_pool(name="vq", bufs=6))
         small = ctx.enter_context(tc.tile_pool(name="small", bufs=16))
         epool = ctx.enter_context(tc.tile_pool(name="epool", bufs=8))
-        spool = ctx.enter_context(tc.tile_pool(name="spool", bufs=S_SB_BUFS))
-        gpool = ctx.enter_context(tc.tile_pool(name="gpool", bufs=5))
+        spool = ctx.enter_context(tc.tile_pool(name="spool", bufs=8))
+        gpool = ctx.enter_context(tc.tile_pool(name="gpool", bufs=7))
         opool = ctx.enter_context(tc.tile_pool(name="opool", bufs=3))
-        ps_s = ctx.enter_context(tc.psum_pool(name="ps_s", bufs=4))
+        ps_s = ctx.enter_context(tc.psum_pool(name="ps_s", bufs=5))
         ps_t = ctx.enter_context(tc.psum_pool(name="ps_t", bufs=2))
         rpool = ctx.enter_context(tc.tile_pool(name="rpool", bufs=4))
-        ps_o = ctx.enter_context(tc.psum_pool(name="ps_o", bufs=2))
-        if MANUAL:
-            ctx.enter_context(tc.manual_schedule())
+        ps_o = ctx.enter_context(tc.psum_pool(name="ps_o", bufs=1))
+        ctx.enter_context(tc.manual_schedule())
 
         ident_b = const.tile([P, P], BF16, name="ident_b")
         ident_f = const.tile([P, P], F32, name="ident_f")
@@ -159,11 +154,13 @@ def tile_window_attention_kernel(tc, kv, q, mask, out):
 
         def add_qk(n, j):
             blk, vw = n // 2, n % 2
+            if n in VECTOR_MASK:
+                chunk[("s", n, j)] = ps_s.tile([P, N], F32, name="s_ps")
             nc.tensor.matmul(
                 out=chunk[("s", n, j)][:],
                 lhsT=blk_t[("q_win", blk)][:, vw * N + j:(vw + 1) * N:4],
                 rhs=blk_t[("k_raw", blk)][:].rearrange("c (h v x) -> c h v x", h=16, v=2)[:, :, vw, :],
-                start=False,
+                start=n in VECTOR_MASK,
                 stop=True,
             )
 
@@ -171,21 +168,17 @@ def tile_window_attention_kernel(tc, kv, q, mask, out):
             w = 2 * (n // 2 // NBD) + n % 2
             src = chunk[("s", n, j)]
             nb = small.tile([P, 1], F32, name="nb")
-            if j in DVE_MASK:
-                s_sb = spool.tile([P, N], F32, name="s_sb")
+            if n in VECTOR_MASK:
+                s_sb = spool.tile([P, N], F32, name="s_sb", tag="s_neg")
                 nc.vector.scalar_tensor_tensor(out=s_sb[:], in0=src[:], scalar=SCALE, in1=blk_t[("m", w)][:, j, :],
                                                op0=ALU.mult, op1=ALU.add)
                 chunk[("s", n, j)] = s_sb
                 nc.vector.tensor_reduce(out=nb[:], in_=s_sb[:], axis=AX.X, op=ALU.max, negate=True)
-            elif FUSED_MAX:
+            else:
                 s_neg = spool.tile([P, N], F32, name="s_neg")
                 nc.vector.tensor_scalar(out=s_neg[:], in0=src[:], scalar1=-SCALE, scalar2=None, op0=ALU.mult,
                                         op1=ALU.min, accum_out=nb[:])
                 chunk[("s", n, j)] = s_neg
-            else:
-                nm = small.tile([P, 1], F32, name="nm")
-                nc.vector.tensor_reduce(out=nm[:], in_=src[:], axis=AX.X, op=ALU.max, negate=True)
-                nc.vector.tensor_scalar_mul(out=nb[:], in0=nm[:], scalar1=SCALE)
             chunk[("nb", n, j)] = nb[:]
 
         def exps(n, half):
@@ -199,7 +192,7 @@ def tile_window_attention_kernel(tc, kv, q, mask, out):
                     in_=chunk[("s", n, j)][:].rearrange("p (m u r) -> p u m r", u=2, r=2),
                     func=AF.Exp,
                     bias=chunk[("nb", n, j)],
-                    scale=(1.0 if j in DVE_MASK else -1.0),
+                    scale=(1.0 if n in VECTOR_MASK else -1.0),
                     accum_out=blk_t[("rs", n // 2)][:, 4 * (n % 2) + j:4 * (n % 2) + j + 1],
                 )
                 chunk[("e", n, j)] = e_sb
@@ -215,7 +208,7 @@ def tile_window_attention_kernel(tc, kv, q, mask, out):
 
         def regroup(n, half):
             if half == 0:
-                unit[("g", n)] = gpool.tile([P, N, 4], BF16, name="grp", align_bytes=64)
+                unit[("g", n)] = gpool.tile([P, N, 4], BF16, name="grp", bufs=4, align_bytes=64)
             nc.scalar.copy(
                 out=unit[("g", n)][:, 256 * half:256 * half + 256, :].bitcast(F32),
                 in_=unit[("et", n, half)][:].rearrange("p u q -> p q u"),
@@ -232,9 +225,12 @@ def tile_window_attention_kernel(tc, kv, q, mask, out):
                 in_=unit[("g", n)][:, lo:hi, :].rearrange("p q t -> p (q t)"),
             )
 
-        def mx_pass(n):
+        def mx_pass(n, spare=False):
             blk, vw = n // 2, n % 2
-            o_ps = ps_o.tile([P, N], F32, name="o_ps")
+            if spare:
+                o_ps = ps_s.tile([P, N], F32, name="o_sp", tag="s_ps")
+            else:
+                o_ps = ps_o.tile([P, N], F32, name="o_ps")
             nc.tensor.matmul_mx(
                 out=o_ps[:],
                 lhsT=blk_t[("v_codes", blk)][:, vw * P:(vw + 1) * P].bitcast(FP8X4),
@@ -265,44 +261,39 @@ def tile_window_attention_kernel(tc, kv, q, mask, out):
                 k = 4 * vw + j
                 nc.tensor.transpose(r_ps[:, j * P:(j + 1) * P], blk_t[("rinv", blk)][:, k:k + 1].to_broadcast([P, P]), ident_f[:])
             r_sb = rpool.tile([P, N], F32, name="r_one")
-            nc.scalar.copy(out=r_sb[:], in_=r_ps[:])
-            unit[("r", n)] = r_sb[:].rearrange("c (j h y) -> c h y j", j=4, h=16)
+            nc.scalar.copy(out=r_sb[:].rearrange("c (p j) -> c p j", j=4), in_=r_ps[:].rearrange("c (j p) -> c p j", j=4))
+            unit[("r", n)] = r_sb[:].rearrange("c (h y j) -> c h y j", h=16, y=8)
 
-        def normalise(n):
+        def normalise(n, rows=slice(0, 16)):
             blk, vw = n // 2, n % 2
-            if vw == 0:
+            if vw == 0 and rows.start == 0:
                 blk_t[("out", blk)] = opool.tile([P, HPIX], F32, name="out_sb")
             out_sb = blk_t[("out", blk)]
             r = unit[("r", n)] if ("r", n) in unit else blk_t[("r", blk)][:, vw]
             nc.vector.tensor_tensor(
-                out=out_sb[:].rearrange("c (h v y j) -> c v h y j", h=16, v=2, y=8)[:, vw],
-                in0=unit[("o_ps", n)][:].rearrange("c (j h y) -> c h y j", j=4, h=16),
-                in1=r,
+                out=out_sb[:].rearrange("c (h v y j) -> c v h y j", h=16, v=2, y=8)[:, vw, rows],
+                in0=unit[("o_ps", n)][:].rearrange("c (j h y) -> c h y j", j=4, h=16)[:, rows],
+                in1=r[:, rows],
                 op=ALU.mult,
             )
 
-        def store(blk):
-            nc.sync.dma_start(out=out_v[blk // NBD, blk % NBD], in_=blk_t[("out", blk)][:])
-
-        def ok(n):
-            return 0 <= n < NUNITS
+        def store(blk, rows=slice(0, 16)):
+            pixels = slice(64 * rows.start, 64 * rows.stop)
+            nc.sync.dma_start(out=out_v[blk // NBD, blk % NBD][:, pixels], in_=blk_t[("out", blk)][:, pixels])
 
         warm = const.tile([P, 1], F32, name="warm")
         nc.vector.memset(warm[:], 0.0)
         nc.scalar.activation(out=warm[:], in_=warm[:], func=AF.Exp)
 
-        load_mask(0)
         load_one("q", 0)
         load_one("k", 0)
+        load_mask(0)
         load_mask(1)
         load_one("v", 0)
         load_blk(1)
         load_blk(2)
         load_mask(2)
         load_mask(3)
-        for half in range(2):
-            mask_transposes(0, half)
-            mask_scale(0, half, half == 0)
         sort_q(0, nc.vector)
 
         for m in range(NUNITS):
@@ -314,92 +305,101 @@ def tile_window_attention_kernel(tc, kv, q, mask, out):
             if vw == 0 and nxt < NBLK:
                 sort_v(nxt, nc.gpsimd)
                 sort_q(nxt, nc.gpsimd)
-            if ok(m):
+            with_mask = m not in VECTOR_MASK
+            if with_mask:
                 add_mask(m, 0)
-                add_qk(m, 0)
-            if ok(m - 1):
+            add_qk(m, 0)
+            if m >= 1:
                 e_transposes(m - 1, 0)
                 regroup(m - 1, 0)
-            if vw == 0 and 1 <= blk < NBLK:
-                v_regroup(blk, VE_ON_ACT)
-            if ok(m):
+            if vw == 0 and 1 <= blk:
+                v_regroup(blk, True)
+            if with_mask:
                 add_mask(m, 1)
-                add_qk(m, 1)
+            add_qk(m, 1)
+            if with_mask:
                 add_mask(m, 2)
                 add_mask(m, 3)
-                add_qk(m, 2)
-            if ok(m - 4):
-                mx_pass(m - 4)
-            if ok(m):
-                add_qk(m, 3)
-            if ok(m - 1):
+            add_qk(m, 2)
+            if m >= 6:
+                mx_pass(m - 6)
+            add_qk(m, 3)
+            if m >= 1:
                 e_transposes(m - 1, 1)
             if m == 0:
                 mask_transposes(1, 0)
+                mask_transposes(1, 1)
+            if m == 1:
+                mask_transposes(0, 1)
+                v_transposes(0)
             if vw == 1 and nxt < NBLK:
                 v_transposes(nxt)
-            if ok(m):
-                row_max(m, 0)
-                row_max(m, 1)
-            if ok(m - 2):
+            row_max(m, 0)
+            if m >= 7:
+                normalise(m - 7)
+                if vw == 0:
+                    store((m - 7) // 2)
+            row_max(m, 1)
+            if m >= 2:
                 quantise_e(m - 2, ALL)
-            if ok(m):
-                row_max(m, 2)
+            row_max(m, 2)
             if vw == 0 and blk >= 1:
                 invert_sums(blk - 1)
                 spread_through_out(blk - 1)
-            if ok(m - 5):
-                normalise(m - 5)
-                if vw == 0:
-                    store((m - 5) // 2)
-            if ok(m):
-                row_max(m, 3)
+            row_max(m, 3)
             if m == 0:
                 sort_v(0, nc.vector)
-            if vw == 0 and 1 <= blk < NBLK:
+            if m == 1:
+                v_regroup(0, False)
+                quantise_v(0)
+            if vw == 0 and 1 <= blk:
                 quantise_v(blk)
             if late_mask is not None:
                 mask_transposes(late_mask, 0)
                 mask_scale(late_mask, 0, False)
-            if ok(m):
-                exps(m, 0)
+            exps(m, 0)
             if m == 0:
                 mask_scale(1, 0, True)
-                mask_transposes(1, 1)
-            if ok(m - 1):
+                mask_transposes(0, 0)
+                mask_scale(1, 1, True)
+                mask_scale(0, 0, False)
+            if m == 1:
+                mask_scale(0, 1, True)
+            if m >= 1:
                 regroup(m - 1, 1)
             if late_mask is not None:
                 mask_transposes(late_mask, 1)
                 mask_scale(late_mask, 1, True)
-            if ok(m):
-                exps(m, 1)
-            if m == 0:
-                mask_scale(1, 1, False)
-                v_transposes(0)
-                v_regroup(0, False)
-                quantise_v(0)
+            exps(m, 1)
 
         z = NUNITS - 1
         last = NBLK - 1
+        upper, lower = slice(0, 8), slice(8, 16)
         e_transposes(z, 0)
         regroup(z, 0)
-        mx_pass(z - 3)
-        e_transposes(z, 1)
+        mx_pass(z - 5, True)
+        mx_pass(z - 4, True)
+        normalise(z - 6)
+        store(last - 3)
         quantise_e(z - 1, ALL)
-        invert_sums(last)
+        normalise(z - 5)
         normalise(z - 4)
         store(last - 2)
-        mx_pass(z - 2)
-        quantise_e(z, (0, 1))
+        mx_pass(z - 3)
+        mx_pass(z - 2, True)
+        e_transposes(z, 1)
         regroup(z, 1)
+        invert_sums(last)
+        quantise_e(z, (0, 1))
         normalise(z - 3)
-        quantise_e(z, (2, 3))
         mx_pass(z - 1)
         spread_on_tensor(z - 1)
         spread_on_tensor(z)
+        quantise_e(z, (2, 3))
         normalise(z - 2)
         store(last - 1)
-        mx_pass(z)
+        mx_pass(z, True)
         normalise(z - 1)
-        normalise(z)
-        store(last)
+        for rows in (upper, lower):
+            normalise(z, rows)
+            store(last, rows)

@@ -24,6 +24,7 @@ SCALE = 1.0 / SQRT_CH
 FLOPS = NUNITS * 2 * (2 * N * N * P)
 
 ALL = (0, 1, 2, 3)
+PARK_ROWS = slice(0, 112, 37)
 VECTOR_MASK = (0,)
 
 
@@ -247,11 +248,18 @@ def tile_window_attention_kernel(tc, kv, q, mask, out):
             nc.vector.reciprocal(out=rinv[:], in_=blk_t[("rs", blk)][:])
             blk_t[("rinv", blk)] = rinv
 
-        def spread_through_out(blk):
-            row = out_v[blk // NBD, blk % NBD, 0]
-            nc.sync.dma_start(out=row.rearrange("(p k) -> p k", k=8), in_=blk_t[("rinv", blk)][:])
+        def park_inverses(blk):
+            rows = out_v[blk // NBD, blk % NBD][PARK_ROWS]
+            nc.sync.dma_start(
+                out=rows.rearrange("r (p k) -> p r k", k=8),
+                in_=blk_t[("rinv", blk)][:].unsqueeze(1).to_broadcast([P, 4, 8]),
+            )
+
+        def spread_inverses(blk):
+            rows = out_v[blk // NBD, blk % NBD][PARK_ROWS]
             r_sb = rpool.tile([P, HPIX], F32, name="r_sb")
-            nc.sync.dma_start(out=r_sb[:], in_=row.partition_broadcast(P))
+            for i in range(4):
+                nc.sync.dma_start(out=r_sb[32 * i:32 * i + 32, :], in_=rows[i].partition_broadcast(32))
             blk_t[("r", blk)] = r_sb[:].rearrange("c (h y v j) -> c v h y j", h=16, y=8, v=2)
 
         def spread_on_tensor(n):
@@ -337,15 +345,16 @@ def tile_window_attention_kernel(tc, kv, q, mask, out):
             row_max(m, 0)
             if m >= 7:
                 normalise(m - 7)
-                if vw == 0:
-                    store((m - 7) // 2)
             row_max(m, 1)
             if m >= 2:
                 quantise_e(m - 2, ALL)
             row_max(m, 2)
             if vw == 0 and blk >= 1:
                 invert_sums(blk - 1)
-                spread_through_out(blk - 1)
+                park_inverses(blk - 1)
+                if m >= 8:
+                    store((m - 7) // 2)
+                spread_inverses(blk - 1)
             row_max(m, 3)
             if m == 0:
                 sort_v(0, nc.vector)

@@ -46,8 +46,8 @@ def tile_window_attention_kernel(tc, kv, q, mask, out):
         spool = ctx.enter_context(tc.tile_pool(name="spool", bufs=8))
         gpool = ctx.enter_context(tc.tile_pool(name="gpool", bufs=7))
         opool = ctx.enter_context(tc.tile_pool(name="opool", bufs=3))
-        ps_s = ctx.enter_context(tc.psum_pool(name="ps_s", bufs=5))
-        ps_t = ctx.enter_context(tc.psum_pool(name="ps_t", bufs=2))
+        ps_s = ctx.enter_context(tc.psum_pool(name="ps_s", bufs=4))
+        ps_t = ctx.enter_context(tc.psum_pool(name="ps_t", bufs=3))
         rpool = ctx.enter_context(tc.tile_pool(name="rpool", bufs=4))
         ps_o = ctx.enter_context(tc.psum_pool(name="ps_o", bufs=1))
         ctx.enter_context(tc.manual_schedule())
@@ -316,15 +316,14 @@ def tile_window_attention_kernel(tc, kv, q, mask, out):
             with_mask = m not in VECTOR_MASK
             if with_mask:
                 add_mask(m, 0)
+                add_mask(m, 1)
             add_qk(m, 0)
+            add_qk(m, 1)
             if m >= 1:
                 e_transposes(m - 1, 0)
                 regroup(m - 1, 0)
             if vw == 0 and 1 <= blk:
                 v_regroup(blk, True)
-            if with_mask:
-                add_mask(m, 1)
-            add_qk(m, 1)
             if with_mask:
                 add_mask(m, 2)
                 add_mask(m, 3)

@@ -23,7 +23,6 @@ SQRT_CH = math.sqrt(128.0)
 SCALE = 1.0 / SQRT_CH
 FLOPS = NUNITS * 2 * (2 * N * N * P)
 
-ALL = (0, 1, 2, 3)
 PARK_ROWS = slice(0, 112, 37)
 VECTOR_MASK = (0,)
 
@@ -40,11 +39,11 @@ def tile_window_attention_kernel(tc, kv, q, mask, out):
         raw = ctx.enter_context(tc.tile_pool(name="raw", bufs=4))
         mraw = ctx.enter_context(tc.tile_pool(name="mraw", bufs=4))
         win = ctx.enter_context(tc.tile_pool(name="win", bufs=4))
-        vq = ctx.enter_context(tc.tile_pool(name="vq", bufs=6))
+        vq = ctx.enter_context(tc.tile_pool(name="vq", bufs=4))
         small = ctx.enter_context(tc.tile_pool(name="small", bufs=16))
         epool = ctx.enter_context(tc.tile_pool(name="epool", bufs=8))
         spool = ctx.enter_context(tc.tile_pool(name="spool", bufs=8))
-        gpool = ctx.enter_context(tc.tile_pool(name="gpool", bufs=7))
+        gpool = ctx.enter_context(tc.tile_pool(name="gpool", bufs=4))
         opool = ctx.enter_context(tc.tile_pool(name="opool", bufs=3))
         ps_s = ctx.enter_context(tc.psum_pool(name="ps_s", bufs=4))
         ps_t = ctx.enter_context(tc.psum_pool(name="ps_t", bufs=3))
@@ -120,24 +119,27 @@ def tile_window_attention_kernel(tc, kv, q, mask, out):
             blk_t[("vt", blk)] = vt
 
         def v_regroup(blk, on_scalar):
-            vg = vq.tile([P, 2, P, 4], BF16, name="vg", align_bytes=64)
+            pair, place = (blk + 1) // 2, 1 - blk % 2
+            if place == 0 or blk == 0:
+                blk_t[("vg", pair)] = vq.tile([P, 2, 2, P, 4], BF16, name="vg", align_bytes=64)
+            vg = blk_t[("vg", pair)][:, place].bitcast(F32)
             src = blk_t[("vt", blk)][:].rearrange("p w u c -> p w c u")
             if on_scalar:
-                nc.scalar.copy(out=vg[:].bitcast(F32), in_=src)
+                nc.scalar.copy(out=vg, in_=src)
             else:
-                nc.vector.tensor_copy(out=vg[:].bitcast(F32), in_=src)
-            blk_t[("vg", blk)] = vg
+                nc.vector.tensor_copy(out=vg, in_=src)
 
-        def quantise_v(blk):
-            v_codes = vq.tile([P, 2 * P], U32, name="v_codes", align_bytes=64)
-            v_scl = vq.tile([P, 2 * P], U8, name="v_scl", align_bytes=64)
+        def quantise_v(pair, places):
+            v_codes = vq.tile([P, 4 * P], U32, name="v_codes", align_bytes=64)
+            v_scl = vq.tile([P, 4 * P], U8, name="v_scl", align_bytes=64)
+            cols = slice(2 * P * places.start, 2 * P * places.stop)
             nc.vector.quantize_mx(
-                out=v_codes[:].bitcast(FP8X4),
-                scales=v_scl[:],
-                in_=blk_t[("vg", blk)][:].rearrange("p w c t -> p (w c t)"),
+                out=v_codes[:, cols].bitcast(FP8X4),
+                scales=v_scl[:, cols],
+                in_=blk_t[("vg", pair)][:, places].rearrange("p b w c t -> p (b w c t)"),
             )
-            blk_t[("v_codes", blk)] = v_codes
-            blk_t[("v_scl", blk)] = v_scl
+            blk_t[("v_codes", pair)] = v_codes
+            blk_t[("v_scl", pair)] = v_scl
 
         def add_mask(n, j):
             w = 2 * (n // 2 // NBD) + n % 2
@@ -165,6 +167,12 @@ def tile_window_attention_kernel(tc, kv, q, mask, out):
                 stop=True,
             )
 
+        def by_pairs(ap):
+            return ap.rearrange("p (m u r) -> p u m r", u=2, r=2)
+
+        def sorted_keys(ap):
+            return ap.rearrange("p (u m r) -> p u m r", u=2, r=2)
+
         def row_max(n, j):
             w = 2 * (n // 2 // NBD) + n % 2
             src = chunk[("s", n, j)]
@@ -177,8 +185,8 @@ def tile_window_attention_kernel(tc, kv, q, mask, out):
                 nc.vector.tensor_reduce(out=nb[:], in_=s_sb[:], axis=AX.X, op=ALU.max, negate=True)
             else:
                 s_neg = spool.tile([P, N], F32, name="s_neg")
-                nc.vector.tensor_scalar(out=s_neg[:], in0=src[:], scalar1=-SCALE, scalar2=None, op0=ALU.mult,
-                                        op1=ALU.min, accum_out=nb[:])
+                nc.vector.tensor_scalar(out=sorted_keys(s_neg[:]), in0=by_pairs(src[:]), scalar1=-SCALE, scalar2=None,
+                                        op0=ALU.mult, op1=ALU.min, accum_out=nb[:])
                 chunk[("s", n, j)] = s_neg
             chunk[("nb", n, j)] = nb[:]
 
@@ -189,8 +197,8 @@ def tile_window_attention_kernel(tc, kv, q, mask, out):
                 j = 2 * half + i
                 e_sb = epool.tile([P, N], BF16, name="e_sb")
                 nc.scalar.activation(
-                    out=e_sb[:].rearrange("p (u m r) -> p u m r", u=2, r=2),
-                    in_=chunk[("s", n, j)][:].rearrange("p (m u r) -> p u m r", u=2, r=2),
+                    out=sorted_keys(e_sb[:]) if n in VECTOR_MASK else e_sb[:],
+                    in_=by_pairs(chunk[("s", n, j)][:]) if n in VECTOR_MASK else chunk[("s", n, j)][:],
                     func=AF.Exp,
                     bias=chunk[("nb", n, j)],
                     scale=(1.0 if n in VECTOR_MASK else -1.0),
@@ -208,36 +216,37 @@ def tile_window_attention_kernel(tc, kv, q, mask, out):
             unit[("et", n, half)] = et
 
         def regroup(n, half):
-            if half == 0:
-                unit[("g", n)] = gpool.tile([P, N, 4], BF16, name="grp", bufs=4, align_bytes=64)
+            if half == 0 and n % 2 == 0:
+                blk_t[("g", n // 2)] = gpool.tile([P, 2 * N, 4], BF16, name="grp", bufs=3, align_bytes=64)
+            lo = N * (n % 2) + 256 * half
             nc.scalar.copy(
-                out=unit[("g", n)][:, 256 * half:256 * half + 256, :].bitcast(F32),
+                out=blk_t[("g", n // 2)][:, lo:lo + 256, :].bitcast(F32),
                 in_=unit[("et", n, half)][:].rearrange("p u q -> p q u"),
             )
 
-        def quantise_e(n, js):
-            if js[0] == 0:
-                unit[("codes", n)] = gpool.tile([P, N], U32, name="codes", align_bytes=64)
-                unit[("scl", n)] = gpool.tile([P, N], U8, name="scl", align_bytes=64)
-            lo, hi = js[0] * P, (js[-1] + 1) * P
+        def quantise_e(blk, lo, hi):
+            if lo == 0:
+                blk_t[("codes", blk)] = gpool.tile([P, 2 * N], U32, name="codes", align_bytes=64)
+                blk_t[("scl", blk)] = gpool.tile([P, 2 * N], U8, name="scl", align_bytes=64)
             nc.vector.quantize_mx(
-                out=unit[("codes", n)][:, lo:hi].bitcast(FP8X4),
-                scales=unit[("scl", n)][:, lo:hi],
-                in_=unit[("g", n)][:, lo:hi, :].rearrange("p q t -> p (q t)"),
+                out=blk_t[("codes", blk)][:, lo:hi].bitcast(FP8X4),
+                scales=blk_t[("scl", blk)][:, lo:hi],
+                in_=blk_t[("g", blk)][:, lo:hi, :].rearrange("p q t -> p (q t)"),
             )
 
         def mx_pass(n, spare=False):
             blk, vw = n // 2, n % 2
+            pair, v_lo = (blk + 1) // 2, (2 * (1 - blk % 2) + vw) * P
             if spare:
                 o_ps = ps_s.tile([P, N], F32, name="o_sp", tag="s_ps")
             else:
                 o_ps = ps_o.tile([P, N], F32, name="o_ps")
             nc.tensor.matmul_mx(
                 out=o_ps[:],
-                lhsT=blk_t[("v_codes", blk)][:, vw * P:(vw + 1) * P].bitcast(FP8X4),
-                lhsT_scale=blk_t[("v_scl", blk)][:, vw * P:(vw + 1) * P],
-                rhs=unit[("codes", n)][:].bitcast(FP8X4),
-                rhs_scale=unit[("scl", n)][:],
+                lhsT=blk_t[("v_codes", pair)][:, v_lo:v_lo + P].bitcast(FP8X4),
+                lhsT_scale=blk_t[("v_scl", pair)][:, v_lo:v_lo + P],
+                rhs=blk_t[("codes", blk)][:, vw * N:(vw + 1) * N].bitcast(FP8X4),
+                rhs_scale=blk_t[("scl", blk)][:, vw * N:(vw + 1) * N],
                 start=True,
                 stop=True,
             )
@@ -259,7 +268,7 @@ def tile_window_attention_kernel(tc, kv, q, mask, out):
             rows = out_v[blk // NBD, blk % NBD][PARK_ROWS]
             r_sb = rpool.tile([P, HPIX], F32, name="r_sb")
             for i in range(4):
-                nc.sync.dma_start(out=r_sb[32 * i:32 * i + 32, :], in_=rows[i].partition_broadcast(32))
+                nc.sync.dma_start(out=r_sb[i:P:4, :], in_=rows[i].partition_broadcast(32))
             blk_t[("r", blk)] = r_sb[:].rearrange("c (h y v j) -> c v h y j", h=16, y=8, v=2)
 
         def spread_on_tensor(n):
@@ -345,8 +354,8 @@ def tile_window_attention_kernel(tc, kv, q, mask, out):
             if m >= 7:
                 normalise(m - 7)
             row_max(m, 1)
-            if m >= 2:
-                quantise_e(m - 2, ALL)
+            if vw == 1 and blk >= 1:
+                quantise_e(blk - 1, 0, 2 * N)
             row_max(m, 2)
             if vw == 0 and blk >= 1:
                 invert_sums(blk - 1)
@@ -359,9 +368,9 @@ def tile_window_attention_kernel(tc, kv, q, mask, out):
                 sort_v(0, nc.vector)
             if m == 1:
                 v_regroup(0, False)
-                quantise_v(0)
-            if vw == 0 and 1 <= blk:
-                quantise_v(blk)
+                quantise_v(0, slice(1, 2))
+            if vw == 0 and 1 <= blk and (blk % 2 == 0 or blk == NBLK - 1):
+                quantise_v((blk + 1) // 2, slice(0, 2 - blk % 2))
             if late_mask is not None:
                 mask_transposes(late_mask, 0)
                 mask_scale(late_mask, 0, False)
@@ -389,7 +398,7 @@ def tile_window_attention_kernel(tc, kv, q, mask, out):
         mx_pass(z - 4, True)
         normalise(z - 6)
         store(last - 3)
-        quantise_e(z - 1, ALL)
+        quantise_e(last, 0, N)
         normalise(z - 5)
         normalise(z - 4)
         store(last - 2)
@@ -398,12 +407,12 @@ def tile_window_attention_kernel(tc, kv, q, mask, out):
         e_transposes(z, 1)
         regroup(z, 1)
         invert_sums(last)
-        quantise_e(z, (0, 1))
+        quantise_e(last, N, N + 256)
         normalise(z - 3)
         mx_pass(z - 1)
         spread_on_tensor(z - 1)
         spread_on_tensor(z)
-        quantise_e(z, (2, 3))
+        quantise_e(last, N + 256, 2 * N)
         normalise(z - 2)
         store(last - 1)
         mx_pass(z, True)

import math
from contextlib import ExitStack

import concourse.mybir as mybir
from concourse.masks import make_identity

F32 = mybir.dt.float32
BF16 = mybir.dt.bfloat16
U32 = mybir.dt.uint32
U8 = mybir.dt.uint8
FP8X4 = mybir.dt.float8_e4m3fn_x4
AF = mybir.ActivationFunctionType
ALU = mybir.AluOpType
AX = mybir.AxisListType

P = 128
NB, HEADS, NWIN, N = 2, 6, 4, 512
NBD = NB * HEADS
NBLK = 2 * NBD
NUNITS = 2 * NBLK
HPIX = 1024
SQRT_CH = math.sqrt(128.0)
SCALE = 1.0 / SQRT_CH
FLOPS = NUNITS * 2 * (2 * N * N * P)

PARK_ROWS = slice(0, 112, 37)
VECTOR_MASK = (0,)


def tile_window_attention_kernel(tc, kv, q, mask, out):
    nc = tc.nc
    q_v = q.rearrange("b (d c) (u h) w -> u (b d) c (h w)", c=P, u=2)
    kv_v = kv.rearrange("s b (d c) (u h) w -> s u (b d) c (h w)", c=P, u=2)
    out_v = out.rearrange("b (d c) (u h) w -> u (b d) c (h w)", c=P, u=2)
    mask_v = mask.rearrange("w (p j) k -> w p j k", j=4)

    with ExitStack() as ctx:
        const = ctx.enter_context(tc.tile_pool(name="const", bufs=1))
        raw = ctx.enter_context(tc.tile_pool(name="raw", bufs=4))
        mraw = ctx.enter_context(tc.tile_pool(name="mraw", bufs=4))
        win = ctx.enter_context(tc.tile_pool(name="win", bufs=4))
        vq = ctx.enter_context(tc.tile_pool(name="vq", bufs=4))
        small = ctx.enter_context(tc.tile_pool(name="small", bufs=16))
        epool = ctx.enter_context(tc.tile_pool(name="epool", bufs=8))
        spool = ctx.enter_context(tc.tile_pool(name="spool", bufs=8))
        gpool = ctx.enter_context(tc.tile_pool(name="gpool", bufs=4))
        opool = ctx.enter_context(tc.tile_pool(name="opool", bufs=3))
        ps_s = ctx.enter_context(tc.psum_pool(name="ps_s", bufs=4))
        ps_t = ctx.enter_context(tc.psum_pool(name="ps_t", bufs=3))
        rpool = ctx.enter_context(tc.tile_pool(name="rpool", bufs=4))
        ps_o = ctx.enter_context(tc.psum_pool(name="ps_o", bufs=1))
        ctx.enter_context(tc.manual_schedule())

        ident_b = const.tile([P, P], BF16, name="ident_b")
        ident_f = const.tile([P, P], F32, name="ident_f")
        make_identity(nc, ident_b[:])
        make_identity(nc, ident_f[:])
        mask_t = const.tile([P, NWIN, 4, N], F32, name="mask_t")

        blk_t = {}
        unit = {}
        chunk = {}

        def load_mask(w):
            m_sb = mraw.tile([P, 4, N], BF16, name="m_sb")
            nc.sync.dma_start(out=m_sb[:], in_=mask_v[w])
            blk_t[("m", w)] = m_sb

        def mask_transposes(w, half):
            m_sb = blk_t[("m", w)]
            mt = ps_t.tile([P, 2, N], BF16, name="mt", tag="tr")
            for ti in range(2):
                for j in range(4):
                    t = 2 * half + ti
                    nc.tensor.transpose(mt[:, ti, j * P:(j + 1) * P], m_sb[:, j, t * P:(t + 1) * P], ident_b[:])
            blk_t[("mt", w, half)] = mt

        def mask_scale(w, half, on_scalar):
            dst = mask_t[:, w, 2 * half:2 * half + 2, :]
            src = blk_t[("mt", w, half)][:]
            if on_scalar:
                nc.scalar.mul(out=dst, in_=src, mul=SQRT_CH)
            else:
                nc.vector.tensor_scalar_mul(out=dst, in0=src, scalar1=SQRT_CH)

        def load_one(what, blk):
            uw, bd = blk // NBD, blk % NBD
            src = {"q": q_v[uw, bd], "k": kv_v[0, uw, bd], "v": kv_v[1, uw, bd]}[what]
            t = raw.tile([P, HPIX], BF16, name=what + "_raw")
            nc.sync.dma_start(out=t[:], in_=src)
            blk_t[(what + "_raw", blk)] = t

        def load_blk(blk):
            for what in ("q", "k", "v"):
                load_one(what, blk)

        def sort_q(blk, eng):
            dst = win.tile([P, 2, 256], F32, name="q_words")
            src = blk_t[("q_raw", blk)][:].bitcast(F32).rearrange("c (h v x) -> c v h x", h=16, v=2)
            for vw in range(2):
                for h in (slice(0, 8), slice(8, 16)):
                    eng.tensor_copy(out=dst[:, vw, :].rearrange("c (h x) -> c h x", h=16)[:, h, :], in_=src[:, vw, h, :])
            blk_t[("q_win", blk)] = dst[:].rearrange("c v n -> c (v n)").bitcast(BF16)

        def sort_v(blk, eng):
            dst = win.tile([P, 2, 2, P], F32, name="v_words")
            src = blk_t[("v_raw", blk)][:].bitcast(F32).rearrange("c (h v x u) -> c v u h x", h=16, v=2, u=2)
            for vw in range(2):
                for u in range(2):
                    eng.tensor_copy(out=dst[:, vw, u, :].rearrange("c (h x) -> c h x", h=16), in_=src[:, vw, u])
            blk_t[("v_words", blk)] = dst

        def v_transposes(blk):
            v_words = blk_t[("v_words", blk)]
            vt = ps_t.tile([P, 2, 2, P], F32, name="vt", tag="tr")
            for vw in range(2):
                for u in range(2):
                    nc.tensor.transpose(vt[:, vw, u, :], v_words[:, vw, u, :], ident_f[:])
            blk_t[("vt", blk)] = vt

        def v_regroup(blk, on_scalar):
            pair, place = (blk + 1) // 2, 1 - blk % 2
            if place == 0 or blk == 0:
                blk_t[("vg", pair)] = vq.tile([P, 2, 2, P, 4], BF16, name="vg", align_bytes=64)
            vg = blk_t[("vg", pair)][:, place].bitcast(F32)
            src = blk_t[("vt", blk)][:].rearrange("p w u c -> p w c u")
            if on_scalar:
                nc.scalar.copy(out=vg, in_=src)
            else:
                nc.vector.tensor_copy(out=vg, in_=src)

        def quantise_v(pair, places):
            v_codes = vq.tile([P, 4 * P], U32, name="v_codes", align_bytes=64)
            v_scl = vq.tile([P, 4 * P], U8, name="v_scl", align_bytes=64)
            cols = slice(2 * P * places.start, 2 * P * places.stop)
            nc.vector.quantize_mx(
                out=v_codes[:, cols].bitcast(FP8X4),
                scales=v_scl[:, cols],
                in_=blk_t[("vg", pair)][:, places].rearrange("p b w c t -> p (b w c t)"),
            )
            blk_t[("v_codes", pair)] = v_codes
            blk_t[("v_scl", pair)] = v_scl

        def add_mask(n, j):
            w = 2 * (n // 2 // NBD) + n % 2
            s_ps = ps_s.tile([P, N], F32, name="s_ps")
            chunk[("s", n, j)] = s_ps
            for t in range(4):
                nc.tensor.matmul(
                    out=s_ps[:, t * P:(t + 1) * P],
                    lhsT=mask_t[:, w, t, j * P:(j + 1) * P],
                    rhs=ident_f[:],
                    is_transpose=True,
                    start=(t == 0),
                    stop=False,
                )

        def add_qk(n, j):
            blk, vw = n // 2, n % 2
            if n in VECTOR_MASK:
                chunk[("s", n, j)] = ps_s.tile([P, N], F32, name="s_ps")
            nc.tensor.matmul(
                out=chunk[("s", n, j)][:],
                lhsT=blk_t[("q_win", blk)][:, vw * N + j:(vw + 1) * N:4],
                rhs=blk_t[("k_raw", blk)][:].rearrange("c (h v x) -> c h v x", h=16, v=2)[:, :, vw, :],
                start=n in VECTOR_MASK,
                stop=True,
            )

        def by_pairs(ap):
            return ap.rearrange("p (m u r) -> p u m r", u=2, r=2)

        def sorted_keys(ap):
            return ap.rearrange("p (u m r) -> p u m r", u=2, r=2)

        def row_max(n, j):
            w = 2 * (n // 2 // NBD) + n % 2
            src = chunk[("s", n, j)]
            nb = small.tile([P, 1], F32, name="nb")
            if n in VECTOR_MASK:
                s_sb = spool.tile([P, N], F32, name="s_sb", tag="s_neg")
                nc.vector.scalar_tensor_tensor(out=s_sb[:], in0=src[:], scalar=SCALE, in1=blk_t[("m", w)][:, j, :],
                                               op0=ALU.mult, op1=ALU.add)
                chunk[("s", n, j)] = s_sb
                nc.vector.tensor_reduce(out=nb[:], in_=s_sb[:], axis=AX.X, op=ALU.max, negate=True)
            else:
                s_neg = spool.tile([P, N], F32, name="s_neg")
                nc.vector.tensor_scalar(out=sorted_keys(s_neg[:]), in0=by_pairs(src[:]), scalar1=-SCALE, scalar2=None,
                                        op0=ALU.mult, op1=ALU.min, accum_out=nb[:])
                chunk[("s", n, j)] = s_neg
            chunk[("nb", n, j)] = nb[:]

        def exps(n, half):
            if half == 0 and n % 2 == 0:
                blk_t[("rs", n // 2)] = small.tile([P, 8], F32, name="rs")
            for i in range(2):
                j = 2 * half + i
                e_sb = epool.tile([P, N], BF16, name="e_sb")
                nc.scalar.activation(
                    out=sorted_keys(e_sb[:]) if n in VECTOR_MASK else e_sb[:],
                    in_=by_pairs(chunk[("s", n, j)][:]) if n in VECTOR_MASK else chunk[("s", n, j)][:],
                    func=AF.Exp,
                    bias=chunk[("nb", n, j)],
                    scale=(1.0 if n in VECTOR_MASK else -1.0),
                    accum_out=blk_t[("rs", n // 2)][:, 4 * (n % 2) + j:4 * (n % 2) + j + 1],
                )
                chunk[("e", n, j)] = e_sb

        def e_transposes(n, half):
            et = ps_t.tile([P, 2, 256], F32, name="et", tag="tr")
            for i in range(2):
                e_sb = chunk[("e", n, 2 * half + i)]
                for u in range(2):
                    nc.tensor.transpose(et[:, u, i * P:(i + 1) * P], e_sb[:].bitcast(F32)[:, u * P:(u + 1) * P],
                                        ident_f[:])
            unit[("et", n, half)] = et

        def regroup(n, half):
            if half == 0 and n % 2 == 0:
                blk_t[("g", n // 2)] = gpool.tile([P, 2 * N, 4], BF16, name="grp", bufs=3, align_bytes=64)
            lo = N * (n % 2) + 256 * half
            nc.scalar.copy(
                out=blk_t[("g", n // 2)][:, lo:lo + 256, :].bitcast(F32),
                in_=unit[("et", n, half)][:].rearrange("p u q -> p q u"),
            )

        def quantise_e(blk, lo, hi):
            if lo == 0:
                blk_t[("codes", blk)] = gpool.tile([P, 2 * N], U32, name="codes", align_bytes=64)
                blk_t[("scl", blk)] = gpool.tile([P, 2 * N], U8, name="scl", align_bytes=64)
            nc.vector.quantize_mx(
                out=blk_t[("codes", blk)][:, lo:hi].bitcast(FP8X4),
                scales=blk_t[("scl", blk)][:, lo:hi],
                in_=blk_t[("g", blk)][:, lo:hi, :].rearrange("p q t -> p (q t)"),
            )

        def mx_pass(n, spare=False):
            blk, vw = n // 2, n % 2
            pair, v_lo = (blk + 1) // 2, (2 * (1 - blk % 2) + vw) * P
            if spare:
                o_ps = ps_s.tile([P, N], F32, name="o_sp", tag="s_ps")
            else:
                o_ps = ps_o.tile([P, N], F32, name="o_ps")
            nc.tensor.matmul_mx(
                out=o_ps[:],
                lhsT=blk_t[("v_codes", pair)][:, v_lo:v_lo + P].bitcast(FP8X4),
                lhsT_scale=blk_t[("v_scl", pair)][:, v_lo:v_lo + P],
                rhs=blk_t[("codes", blk)][:, vw * N:(vw + 1) * N].bitcast(FP8X4),
                rhs_scale=blk_t[("scl", blk)][:, vw * N:(vw + 1) * N],
                start=True,
                stop=True,
            )
            unit[("o_ps", n)] = o_ps

        def invert_sums(blk):
            rinv = small.tile([P, 8], F32, name="rinv")
            nc.vector.reciprocal(out=rinv[:], in_=blk_t[("rs", blk)][:])
            blk_t[("rinv", blk)] = rinv

        def park_inverses(blk):
            rows = out_v[blk // NBD, blk % NBD][PARK_ROWS]
            nc.sync.dma_start(
                out=rows.rearrange("r (p k) -> p r k", k=8),
                in_=blk_t[("rinv", blk)][:].unsqueeze(1).to_broadcast([P, 4, 8]),
            )

        def spread_inverses(blk):
            rows = out_v[blk // NBD, blk % NBD][PARK_ROWS]
            r_sb = rpool.tile([P, HPIX], F32, name="r_sb")
            for i in range(4):
                nc.sync.dma_start(out=r_sb[i:P:4, :], in_=rows[i].partition_broadcast(32))
            blk_t[("r", blk)] = r_sb[:].rearrange("c (h y v j) -> c v h y j", h=16, y=8, v=2)

        def spread_on_tensor(n):
            blk, vw = n // 2, n % 2
            r_ps = ps_s.tile([P, N], F32, name="r_ps", tag="s_ps")
            for j in range(4):
                k = 4 * vw + j
                nc.tensor.transpose(r_ps[:, j * P:(j + 1) * P], blk_t[("rinv", blk)][:, k:k + 1].to_broadcast([P, P]), ident_f[:])
            r_sb = rpool.tile([P, N], F32, name="r_one")
            nc.scalar.copy(out=r_sb[:].rearrange("c (p j) -> c p j", j=4), in_=r_ps[:].rearrange("c (j p) -> c p j", j=4))
            unit[("r", n)] = r_sb[:].rearrange("c (h y j) -> c h y j", h=16, y=8)

        def normalise(n, rows=slice(0, 16)):
            blk, vw = n // 2, n % 2
            if vw == 0 and rows.start == 0:
                blk_t[("out", blk)] = opool.tile([P, HPIX], F32, name="out_sb")
            out_sb = blk_t[("out", blk)]
            r = unit[("r", n)] if ("r", n) in unit else blk_t[("r", blk)][:, vw]
            nc.vector.tensor_tensor(
                out=out_sb[:].rearrange("c (h v y j) -> c v h y j", h=16, v=2, y=8)[:, vw, rows],
                in0=unit[("o_ps", n)][:].rearrange("c (j h y) -> c h y j", j=4, h=16)[:, rows],
                in1=r[:, rows],
                op=ALU.mult,
            )

        def store(blk, rows=slice(0, 16)):
            pixels = slice(64 * rows.start, 64 * rows.stop)
            nc.sync.dma_start(out=out_v[blk // NBD, blk % NBD][:, pixels], in_=blk_t[("out", blk)][:, pixels])

        warm = const.tile([P, 1], F32, name="warm")
        nc.vector.memset(warm[:], 0.0)
        nc.scalar.activation(out=warm[:], in_=warm[:], func=AF.Exp)

        load_one("q", 0)
        load_one("k", 0)
        load_mask(0)
        load_mask(1)
        load_one("v", 0)
        load_blk(1)
        load_blk(2)
        load_mask(2)
        load_mask(3)
        sort_q(0, nc.vector)

        for m in range(NUNITS):
            blk, vw = m // 2, m % 2
            nxt = blk + 1
            late_mask = {4: 2, 6: 3}.get(m)
            if vw == 0 and 1 <= blk and blk + 2 < NBLK:
                load_blk(blk + 2)
            if vw == 0 and nxt < NBLK:
                sort_v(nxt, nc.gpsimd)
                sort_q(nxt, nc.gpsimd)
            with_mask = m not in VECTOR_MASK
            if with_mask:
                add_mask(m, 0)
                add_mask(m, 1)
            add_qk(m, 0)
            add_qk(m, 1)
            if m >= 1:
                e_transposes(m - 1, 0)
                regroup(m - 1, 0)
            if vw == 0 and 1 <= blk:
                v_regroup(blk, True)
            if with_mask:
                add_mask(m, 2)
                add_mask(m, 3)
            add_qk(m, 2)
            if m >= 6:
                mx_pass(m - 6)
            add_qk(m, 3)
            if m >= 1:
                e_transposes(m - 1, 1)
            if m == 0:
                mask_transposes(1, 0)
                mask_transposes(1, 1)
            if m == 1:
                mask_transposes(0, 1)
                v_transposes(0)
            if vw == 1 and nxt < NBLK:
                v_transposes(nxt)
            row_max(m, 0)
            if m >= 7:
                normalise(m - 7)
            row_max(m, 1)
            if vw == 1 and blk >= 1:
                quantise_e(blk - 1, 0, 2 * N)
            row_max(m, 2)
            if vw == 0 and blk >= 1:
                invert_sums(blk - 1)
                park_inverses(blk - 1)
                if m >= 8:
                    store((m - 7) // 2)
                spread_inverses(blk - 1)
            row_max(m, 3)
            if m == 0:
                sort_v(0, nc.vector)
            if m == 1:
                v_regroup(0, False)
                quantise_v(0, slice(1, 2))
            if vw == 0 and 1 <= blk and (blk % 2 == 0 or blk == NBLK - 1):
                quantise_v((blk + 1) // 2, slice(0, 2 - blk % 2))
            if late_mask is not None:
                mask_transposes(late_mask, 0)
                mask_scale(late_mask, 0, False)
            exps(m, 0)
            if m == 0:
                mask_scale(1, 0, True)
                mask_transposes(0, 0)
                mask_scale(1, 1, True)
                mask_scale(0, 0, False)
            if m == 1:
                mask_scale(0, 1, True)
            if m >= 1:
                regroup(m - 1, 1)
            if late_mask is not None:
                mask_transposes(late_mask, 1)
                mask_scale(late_mask, 1, True)
            exps(m, 1)

        z = NUNITS - 1
        last = NBLK - 1
        upper, lower = slice(0, 8), slice(8, 16)
        e_transposes(z, 0)
        regroup(z, 0)
        mx_pass(z - 5, True)
        mx_pass(z - 4, True)
        normalise(z - 6)
        store(last - 3)
        quantise_e(last, 0, N)
        normalise(z - 5)
        normalise(z - 4)
        store(last - 2)
        mx_pass(z - 3)
        mx_pass(z - 2, True)
        e_transposes(z, 1)
        regroup(z, 1)
        invert_sums(last)
        quantise_e(last, N, N + 256)
        normalise(z - 3)
        mx_pass(z - 1)
        spread_on_tensor(z - 1)
        spread_on_tensor(z)
        quantise_e(last, N + 256, 2 * N)
        normalise(z - 2)
        store(last - 1)
        mx_pass(z, True)
        normalise(z - 1)
        for rows in (upper, lower):
            normalise(z, rows)
            store(last, rows)
